import numpy as np
import ml_dtypes


def mxq(x, axis, fmt="e4m3"):
    dtype, down = {"e4m3": (ml_dtypes.float8_e4m3fn, 7), "e5m2": (ml_dtypes.float8_e5m2, 14)}[fmt]
    v = np.moveaxis(np.asarray(x, np.float32).astype(ml_dtypes.bfloat16).astype(np.float64), axis, -1)
    blocks = v.reshape(v.shape[:-1] + (-1, 32))
    amax = np.abs(blocks).max(-1, keepdims=True)
    byte = np.maximum(np.where(amax > 0, np.frexp(amax)[1] - 1 + 127, 0) - down, 1)
    scale = np.exp2(byte - 127.0)
    codes = (blocks / scale).astype(np.float32).astype(dtype).astype(np.float64)
    return np.moveaxis((codes * scale).reshape(v.shape), -1, axis)


WIDE = False


def mx_kscale(k):
    if not WIDE:
        return np.ones(k)
    levels = np.array([10, -10, 5, -5, 0])
    if k % 512:
        return np.exp2(np.random.permutation(np.resize(levels, k // 32))).repeat(32)
    a = np.empty((k // 512, 16))
    for p in range(k // 512):
        a[p, :8] = np.random.permutation(np.resize(levels, 8))
        for g in range(8):
            far = levels[np.abs(levels - a[p, g]) >= 10]
            a[p, g + 8] = far[np.random.randint(len(far))]
    return np.exp2(a.ravel()).repeat(32)


BF16 = ml_dtypes.bfloat16


def bf(x):
    return np.asarray(x, np.float32).astype(BF16)


def f64(x):
    return np.asarray(x).astype(np.float64)


B, K, G, D, FF, F, P, H = 128, 32, 128, 1024, 512, 2048, 7, 8
NC = K * G
EPS = 1e-5


def layernorm(x, g, b):
    m = x.mean(-1, keepdims=True)
    v = ((x - m) ** 2).mean(-1, keepdims=True)
    return (x - m) / np.sqrt(v + EPS) * g + b


def setup_inputs():
    n = np.random.standard_normal
    s, t = mx_kscale(FF), mx_kscale(D)
    return {
        "ff_hid": bf(np.maximum(n((B, K, FF)), 0.0) * s),
        "tgt": bf(n((B, K, D))),
        "w2": bf(n((FF, D)) / np.sqrt(FF) / s[:, None]),
        "b2": bf(0.1 * n(D)),
        "g3": bf((1.0 + 0.1 * n(D)) * t),
        "be3": bf(0.1 * n(D) * t),
        "dup_pool": bf(n((K, D, G)) / np.sqrt(D) / t[None, :, None]),
        "dup_bias": bf(0.2 * n(NC)),
    }


def reference(ff_hid, tgt, w2, b2, g3, be3, dup_pool, dup_bias):
    ff = (mxq(f64(ff_hid), 2, "e4m3") @ mxq(f64(w2), 0, "e4m3")) + f64(b2)
    h = layernorm(f64(tgt) + ff, f64(g3), f64(be3))
    out_extrap = (mxq(h, 2, "e4m3").transpose(1, 0, 2) @ mxq(f64(dup_pool), 1, "e4m3")).transpose(1, 0, 2)
    return out_extrap.reshape(B, -1)[:, :NC] + f64(dup_bias)

@@ -1,0 +1,358 @@
+from contextlib import ExitStack
+
+import concourse.mybir as mybir
+from concourse.masks import make_identity
+
+F32 = mybir.dt.float32
+BF16 = mybir.dt.bfloat16
+U32 = mybir.dt.uint32
+U8 = mybir.dt.uint8
+FP8X4 = mybir.dt.float8_e4m3fn_x4
+ALU = mybir.AluOpType
+ACT = mybir.ActivationFunctionType
+
+P = 128
+B, K, G, D, FF = 128, 32, 128, 1024, 512
+EPS = 1e-5
+FLOPS = 2 * B * K * FF * D + 2 * B * K * D * G
+DUP_ON_GPSIMD = True
+XH_ON_VECTOR_FROM = K
+AF_ON_VECTOR_EVERY = 64
+
+
+def tile_mldecoder_pb_t_kernel(tc, ff_hid, tgt, w2, b2, g3, be3, dup_pool, dup_bias, out):
+    nc = tc.nc
+    with ExitStack() as ctx:
+        const = ctx.enter_context(tc.tile_pool(name="const", bufs=1))
+        loads = ctx.enter_context(tc.tile_pool(name="loads", bufs=5))
+        work = ctx.enter_context(tc.tile_pool(name="work", bufs=2))
+        small = ctx.enter_context(tc.tile_pool(name="small", bufs=8))
+        psum = ctx.enter_context(tc.psum_pool(name="psum", bufs=2))
+        ctx.enter_context(tc.manual_schedule())
+
+        ffh_t, tgt_t, dup_t = {}, {}, {}
+        ffT_t, ffg_t, ff_q = {}, {}, {}
+        u_of, s1_of, s0_of, negm_of, ss_of, std_of, rstd_of, nb_of = {}, {}, {}, {}, {}, {}, {}, {}
+        z_of, zT_of, hp_of, hg_of, h_q, dg_of, d_q, o2_t = {}, {}, {}, {}, {}, {}, {}, {}
+
+        def load_ffh(p):
+            ffh = loads.tile([P, 2, FF], BF16, tag="ffh", bufs=4)
+            nc.sync.dma_start(out=ffh[:], in_=ff_hid[:, 2 * p : 2 * p + 2, :])
+            ffh_t[p] = ffh
+
+        def load_tgt(p):
+            tg = loads.tile([P, 2, D], BF16, tag="tg", bufs=5)
+            nc.sync.dma_start(out=tg[:], in_=tgt[:, 2 * p : 2 * p + 2, :])
+            tgt_t[p] = tg
+
+        def load_dup(p):
+            dr_t = loads.tile([P, 2, 2, 4 * G], BF16, tag="dr", bufs=5)
+            nc.sync.dma_start(out=dr_t[:], in_=dup_pool[2 * p : 2 * p + 2].rearrange("k (a p t) g -> p k a (t g)", p=P, t=4))
+            dup_t[p] = dr_t
+
+        gb_raw = const.tile([P, 512], BF16)
+        nc.vector.memset(gb_raw[:], 0.0)
+        nc.sync.dma_start(out=gb_raw[0:2, :], in_=g3.rearrange("(a i) -> a i", a=2))
+        nc.sync.dma_start(out=gb_raw[2:4, :], in_=be3.rearrange("(a i) -> a i", a=2))
+        load_ffh(0)
+        w2raw = const.tile([P, 4, D], BF16)
+        nc.sync.dma_start(out=w2raw[:], in_=w2.rearrange("(p j) c -> p j c", j=4))
+        b2row = const.tile([P, D], BF16)
+        nc.sync.dma_start(out=b2row[:], in_=b2.partition_broadcast(P))
+        b2bc = const.tile([P, D], BF16)
+        nc.gpsimd.tensor_scalar(
+            out=b2bc[:].rearrange("p (a t m) -> p a t m", a=2, t=4),
+            in0=b2row[:].rearrange("p (a m t) -> p a t m", a=2, t=4),
+            scalar1=1.0, scalar2=0.0, op0=ALU.mult, op1=ALU.add,
+        )
+        load_tgt(0)
+        load_ffh(1)
+        load_tgt(1)
+        load_dup(0)
+        load_dup(1)
+        load_ffh(2)
+        load_tgt(2)
+        load_dup(2)
+        dbias = const.tile([P, K * G], BF16)
+
+        eps_t = const.tile([P, 1], F32)
+        nc.vector.memset(eps_t[:], EPS)
+        warm = const.tile([P, 1], F32)
+        nc.scalar.activation(out=warm[:], in_=eps_t[:], func=ACT.Abs_reciprocal_sqrt)
+        ident_f = const.tile([P, P], F32)
+        make_identity(nc, ident_f[:])
+        ident_b = const.tile([P, P], BF16)
+        make_identity(nc, ident_b[:])
+
+        w2c = const.tile([P, D], U32, align_bytes=64)
+        w2s = const.tile([P, D], U8, align_bytes=64)
+        w2g = const.tile([P, 2, 512, 4], BF16, align_bytes=64)
+
+        def regroup_w2():
+            nc.vector.tensor_copy(
+                out=w2g[:, 0].rearrange("p (t m) j -> p t m j", t=4),
+                in_=w2raw[:, :, 0:512].rearrange("p j (m t) -> p t m j", t=4),
+            )
+            nc.scalar.copy(
+                out=w2g[:, 1].rearrange("p (t m) j -> p t m j", t=4),
+                in_=w2raw[:, :, 512:1024].rearrange("p j (m t) -> p t m j", t=4),
+            )
+
+        def quant_w2(h):
+            nc.vector.quantize_mx(
+                out=w2c[:, 512 * h : 512 * h + 512].bitcast(FP8X4),
+                scales=w2s[:, 512 * h : 512 * h + 512],
+                in_=w2g[:, h].rearrange("p c t -> p (c t)"),
+            )
+
+        gb = const.tile([P, 4, 4], F32)
+
+        def gain_shift_columns():
+            gb_ps = psum.tile([P, 4, P], BF16, tag="o2", bufs=2)
+            for t in range(4):
+                nc.tensor.transpose(gb_ps[:, t, :], gb_raw[:, t:512:4], ident_b[:])
+            nc.vector.tensor_copy(out=gb[:], in_=gb_ps[:, :, 0:4])
+
+        def t_ff(p):
+            ffT = psum.tile([P, 2, 2, P], F32, tag="ffT", bufs=1)
+            for j in range(2):
+                k = 2 * p + j
+                words = ffh_t[p][:, j, :].bitcast(F32)
+                for u in range(2):
+                    nc.tensor.transpose(ffT[:, j, u, :], words[:, u : 2 * P : 2], ident_f[:])
+            ffT_t[p] = ffT
+
+        def c_ff(p):
+            ffg = work.tile([P, 2, P, 4], BF16, tag="ffg", bufs=2, align_bytes=64)
+            nc.scalar.copy(out=ffg[:].bitcast(F32), in_=ffT_t[p][:].rearrange("p j u b -> p j b u"))
+            ffg_t[p] = ffg
+
+        def q_ff(p):
+            ffc = work.tile([P, 2 * P], U32, tag="ffc", bufs=3, align_bytes=64)
+            ffs = work.tile([P, 2 * P], U8, tag="ffs", bufs=3, align_bytes=64)
+            nc.vector.quantize_mx(
+                out=ffc[:].bitcast(FP8X4), scales=ffs[:], in_=ffg_t[p][:].rearrange("p j b t -> p (j b t)")
+            )
+            ff_q[p] = (ffc, ffs)
+
+        def tb(k):
+            u_t = work.tile([P, D], F32, tag="u", bufs=7)
+            nc.vector.tensor_tensor(
+                out=u_t[:].rearrange("p (a t m) -> p a t m", a=2, t=4),
+                in0=tgt_t[k // 2][:, k % 2, :].rearrange("p (a m t) -> p a t m", a=2, t=4),
+                in1=b2bc[:].rearrange("p (a t m) -> p a t m", a=2, t=4),
+                op=ALU.add,
+            )
+            u_of[k] = u_t
+
+        def m1(k):
+            ffc, ffs = ff_q[k // 2]
+            cols = slice(P * (k % 2), P * (k % 2) + P)
+            banks = []
+            for h in range(2):
+                s1 = psum.tile([P, 512], F32, tag="s1", bufs=3)
+                n_cols = slice(512 * h, 512 * h + 512)
+                nc.tensor.matmul_mx(
+                    out=s1[:],
+                    lhsT=ffc[:, cols].bitcast(FP8X4),
+                    lhsT_scale=ffs[:, cols],
+                    rhs=w2c[:, n_cols].bitcast(FP8X4),
+                    rhs_scale=w2s[:, n_cols],
+                    start=True,
+                    stop=True,
+                )
+                banks.append(s1)
+            s1_of[k] = banks
+
+        def p1(k):
+            s0 = small.tile([P, 2], F32, tag="s0")
+            for h in range(2):
+                n_cols = slice(512 * h, 512 * h + 512)
+                nc.vector.scalar_tensor_tensor(
+                    out=u_of[k][:, n_cols], in0=s1_of[k][h][:], scalar=1.0, in1=u_of[k][:, n_cols],
+                    op0=ALU.mult, op1=ALU.add, accum_out=s0[:, h : h + 1],
+                )
+            s0_of[k] = s0
+
+        def nm(k):
+            negm = small.tile([P, 1], F32, tag="negm")
+            s0 = s0_of[k]
+            nc.vector.tensor_scalar(
+                out=negm[:], in0=s0[:, 0:1], scalar1=s0[:, 1:2], scalar2=-1.0 / D, op0=ALU.add, op1=ALU.mult
+            )
+            negm_of[k] = negm
+
+        def sq(k):
+            junk = work.tile([P, D], BF16, tag="junk", bufs=1)
+            ss = small.tile([P, 1], F32, tag="ss")
+            nc.scalar.activation(
+                out=junk[:], in_=u_of[k][:], func=ACT.Square, bias=negm_of[k][:], scale=1.0, accum_out=ss[:]
+            )
+            ss_of[k] = ss
+
+        def sr(k):
+            rstd = small.tile([P, 1], F32, tag="rstd")
+            nc.scalar.activation(
+                out=rstd[:], in_=ss_of[k][:], func=ACT.Abs_reciprocal_sqrt, bias=eps_t[:], scale=1.0 / D
+            )
+            rstd_of[k] = rstd
+
+        def nbias(k):
+            nb = small.tile([P, 1], F32, tag="nb")
+            nc.scalar.activation(out=nb[:], in_=negm_of[k][:], func=ACT.Copy, scale=rstd_of[k][:])
+            nb_of[k] = nb
+
+        def xh(k):
+            z = work.tile([P, D], F32, tag="z", bufs=2)
+            if k >= XH_ON_VECTOR_FROM:
+                nc.vector.tensor_scalar(
+                    out=z[:], in0=u_of[k][:], scalar1=negm_of[k][:], scalar2=rstd_of[k][:], op0=ALU.add, op1=ALU.mult
+                )
+            else:
+                nc.scalar.activation(
+                    out=z[:], in_=u_of[k][:], func=ACT.Identity, bias=nb_of[k][:], scale=rstd_of[k][:]
+                )
+            z_of[k] = z
+
+        def tz(k):
+            banks = []
+            for a in range(2):
+                zT = psum.tile([P, 4, P], F32, tag="zT", bufs=2)
+                for t in range(4):
+                    c = 4 * a + t
+                    nc.tensor.transpose(zT[:, t, :], z_of[k][:, P * c : P * c + P], ident_f[:])
+                banks.append(zT)
+            zT_of[k] = banks
+
+        def af(k, a):
+            if a == 0:
+                hp_new = work.tile([P, 8, P], BF16, tag="hp", bufs=2)
+                hp_of[k] = hp_new
+            for t in range(4):
+                c = 4 * a + t
+                nc.scalar.activation(
+                    out=hp_of[k][:, c, :], in_=zT_of[k][a][:, t, :], func=ACT.Identity,
+                    bias=gb[:, t, 2 + a : 3 + a], scale=gb[:, t, a : a + 1],
+                )
+
+        def rg(k):
+            hg = work.tile([P, 2, P, 4], BF16, tag="hg", bufs=3, align_bytes=64)
+            nc.vector.tensor_copy(
+                out=hg[:].rearrange("p a (c i) t -> p a c t i", i=4),
+                in_=hp_of[k][:].rearrange("p (a t) (c i) -> p a c t i", t=4, i=4),
+            )
+            hg_of[k] = hg
+
+        def qh(k):
+            hc = work.tile([P, 2 * P], U32, tag="hc", bufs=3, align_bytes=64)
+            hs = work.tile([P, 2 * P], U8, tag="hs", bufs=3, align_bytes=64)
+            nc.vector.quantize_mx(
+                out=hc[:].bitcast(FP8X4), scales=hs[:], in_=hg_of[k][:].rearrange("p a b t -> p (a b t)")
+            )
+            h_q[k] = (hc, hs)
+
+        def dr(k):
+            dg = work.tile([P, 2, G, 4], BF16, tag="dg", bufs=2, align_bytes=64)
+            if DUP_ON_GPSIMD:
+                nc.gpsimd.tensor_scalar(
+                    out=dg[:], in0=dup_t[k // 2][:, k % 2].rearrange("p a (t g) -> p a g t", t=4),
+                    scalar1=1.0, scalar2=0.0, op0=ALU.mult, op1=ALU.add,
+                )
+            else:
+                nc.vector.tensor_copy(
+                    out=dg[:], in_=dup_t[k // 2][:, k % 2].rearrange("p a (t g) -> p a g t", t=4)
+                )
+            dg_of[k] = dg
+
+        def qd(k):
+            dc = work.tile([P, 2 * G], U32, tag="dc", bufs=6, align_bytes=64)
+            ds = work.tile([P, 2 * G], U8, tag="ds", bufs=6, align_bytes=64)
+            nc.vector.quantize_mx(
+                out=dc[:].bitcast(FP8X4), scales=ds[:], in_=dg_of[k][:].rearrange("p a g t -> p (a g t)")
+            )
+            d_q[k] = (dc, ds)
+
+        def m2(k):
+            if k % 4 == 0:
+                o2_new = psum.tile([P, 4 * G], F32, tag="o2", bufs=2)
+                o2_t[k // 4] = o2_new
+            hc, hs = h_q[k]
+            dc, ds = d_q[k]
+            for a in range(2):
+                sl = slice(P * a, P * a + P)
+                nc.tensor.matmul_mx(
+                    out=o2_t[k // 4][:, G * (k % 4) : G * (k % 4) + G],
+                    lhsT=hc[:, sl].bitcast(FP8X4),
+                    lhsT_scale=hs[:, sl],
+                    rhs=dc[:, sl].bitcast(FP8X4),
+                    rhs_scale=ds[:, sl],
+                    start=(a == 0),
+                    stop=(a == 1),
+                )
+
+        def oa(g):
+            o_cols = slice(4 * G * g, 4 * G * g + 4 * G)
+            ob = work.tile([P, 4 * G], F32, tag="ob", bufs=2)
+            nc.vector.tensor_tensor(out=ob[:], in0=o2_t[g][:], in1=dbias[:, o_cols], op=ALU.add)
+            nc.sync.dma_start(out=out[:, o_cols], in_=ob[:])
+
+        def tok(k):
+            return 0 <= k < K
+
+        gain_shift_columns()
+        t_ff(0)
+        c_ff(0)
+        q_ff(0)
+        regroup_w2()
+        quant_w2(0)
+        for n in range(-3, K + 8):
+            if n % 2 == 0:
+                p_new = (n + 8) // 2
+                if 3 <= p_new < K // 2:
+                    load_ffh(p_new)
+                    load_tgt(p_new)
+                    load_dup(p_new)
+            if n == 0:
+                nc.sync.dma_start(out=dbias[:], in_=dup_bias.partition_broadcast(P))
+            if tok(n):
+                p1(n)
+            if tok(n - 7) and (n - 7) % 4 == 3:
+                oa((n - 7) // 4)
+            if tok(n - 4):
+                af(n - 4, 0)
+            if tok(n - 3):
+                xh(n - 3)
+            if tok(n - 2):
+                sr(n - 2)
+            if tok(n + 1):
+                m1(n + 1)
+            if tok(n - 6):
+                m2(n - 6)
+            if tok(n - 4):
+                af(n - 4, 1)
+            if tok(n + 2):
+                tb(n + 2)
+            if n == -2:
+                quant_w2(1)
+            if tok(n):
+                nm(n)
+            if tok(n - 3):
+                tz(n - 3)
+            if n >= 0 and n % 2 == 0 and tok(n + 2):
+                q_ff((n + 2) // 2)
+            if tok(n - 5):
+                qh(n - 5)
+            if tok(n - 4):
+                rg(n - 4)
+            if tok(n - 1):
+                sq(n - 1)
+            if tok(n - 2):
+                nbias(n - 2)
+            if tok(n - 2):
+                qd(n - 2)
+            if tok(n):
+                dr(n)
+            if n >= -2 and n % 2 == 0 and tok(n + 4):
+                t_ff((n + 4) // 2)
+            if n >= -1 and (n + 3) % 2 == 0 and tok(n + 3):
+                c_ff((n + 3) // 2)

@@ -58,13 +58,10 @@ def tile_mldecoder_pb_t_kernel(tc, ff_hid, tgt, w2, b2, g3, be3, dup_pool, dup_b
         w2raw = const.tile([P, 4, D], BF16)
         nc.sync.dma_start(out=w2raw[:], in_=w2.rearrange("(p j) c -> p j c", j=4))
         b2row = const.tile([P, D], BF16)
-        nc.sync.dma_start(out=b2row[:], in_=b2.partition_broadcast(P))
-        b2bc = const.tile([P, D], BF16)
-        nc.gpsimd.tensor_scalar(
-            out=b2bc[:].rearrange("p (a t m) -> p a t m", a=2, t=4),
-            in0=b2row[:].rearrange("p (a m t) -> p a t m", a=2, t=4),
-            scalar1=1.0, scalar2=0.0, op0=ALU.mult, op1=ALU.add,
-        )
+        nc.vector.memset(b2row[:], 0.0)
+        nc.sync.dma_start(out=b2row[0:1, :], in_=b2.rearrange("(o d) -> o d", o=1))
+        ones = const.tile([P, P], BF16)
+        nc.vector.memset(ones[:], 1.0)
         load_tgt(0)
         load_ffh(1)
         load_tgt(1)
@@ -113,6 +110,15 @@ def tile_mldecoder_pb_t_kernel(tc, ff_hid, tgt, w2, b2, g3, be3, dup_pool, dup_b
                 nc.tensor.transpose(gb_ps[:, t, :], gb_raw[:, t:512:4], ident_b[:])
             nc.vector.tensor_copy(out=gb[:], in_=gb_ps[:, :, 0:4])
 
+        b2bc = psum.tile([P, 2, 4, P], BF16, tag="b2", bufs=1)
+
+        def spread_b2():
+            for a in range(2):
+                for t in range(4):
+                    nc.tensor.matmul(
+                        b2bc[:, a, t, :], lhsT=ones[:], rhs=b2row[:, 512 * a + t : 512 * a + 512 : 4], start=True, stop=True
+                    )
+
         def t_ff(p):
             ffT = psum.tile([P, 2, 2, P], F32, tag="ffT", bufs=1)
             for j in range(2):
@@ -139,8 +145,8 @@ def tile_mldecoder_pb_t_kernel(tc, ff_hid, tgt, w2, b2, g3, be3, dup_pool, dup_b
             u_t = work.tile([P, D], F32, tag="u", bufs=7)
             nc.vector.tensor_tensor(
                 out=u_t[:].rearrange("p (a t m) -> p a t m", a=2, t=4),
-                in0=tgt_t[k // 2][:, k % 2, :].rearrange("p (a m t) -> p a t m", a=2, t=4),
-                in1=b2bc[:].rearrange("p (a t m) -> p a t m", a=2, t=4),
+                in0=b2bc[:],
+                in1=tgt_t[k // 2][:, k % 2, :].rearrange("p (a m t) -> p a t m", a=2, t=4),
                 op=ALU.add,
             )
             u_of[k] = u_t
@@ -150,7 +156,7 @@ def tile_mldecoder_pb_t_kernel(tc, ff_hid, tgt, w2, b2, g3, be3, dup_pool, dup_b
             cols = slice(P * (k % 2), P * (k % 2) + P)
             banks = []
             for h in range(2):
-                s1 = psum.tile([P, 512], F32, tag="s1", bufs=3)
+                s1 = psum.tile([P, 512], F32, tag="s1", bufs=2)
                 n_cols = slice(512 * h, 512 * h + 512)
                 nc.tensor.matmul_mx(
                     out=s1[:],
@@ -301,6 +307,7 @@ def tile_mldecoder_pb_t_kernel(tc, ff_hid, tgt, w2, b2, g3, be3, dup_pool, dup_b
 
         gain_shift_columns()
         t_ff(0)
+        spread_b2()
         c_ff(0)
         q_ff(0)
         regroup_w2()

@@ -16,7 +16,8 @@ B, K, G, D, FF = 128, 32, 128, 1024, 512
 EPS = 1e-5
 FLOPS = 2 * B * K * FF * D + 2 * B * K * D * G
 DUP_ON_GPSIMD = True
-XH_ON_VECTOR_FROM = K
+XH_ON_VECTOR_FROM = K - 3
+AF_SHARED_FROM = K - 4
 AF_ON_VECTOR_EVERY = 64
 
 
@@ -42,7 +43,11 @@ def tile_mldecoder_pb_t_kernel(tc, ff_hid, tgt, w2, b2, g3, be3, dup_pool, dup_b
 
         def load_tgt(p):
             tg = loads.tile([P, 2, D], BF16, tag="tg", bufs=5)
-            nc.sync.dma_start(out=tg[:], in_=tgt[:, 2 * p : 2 * p + 2, :])
+            if p == 0:
+                for j in range(2):
+                    nc.sync.dma_start(out=tg[:, j, :], in_=tgt[:, j, :])
+            else:
+                nc.sync.dma_start(out=tg[:], in_=tgt[:, 2 * p : 2 * p + 2, :])
             tgt_t[p] = tg
 
         def load_dup(p):
@@ -50,19 +55,27 @@ def tile_mldecoder_pb_t_kernel(tc, ff_hid, tgt, w2, b2, g3, be3, dup_pool, dup_b
             nc.sync.dma_start(out=dr_t[:], in_=dup_pool[2 * p : 2 * p + 2].rearrange("k (a p t) g -> p k a (t g)", p=P, t=4))
             dup_t[p] = dr_t
 
-        gb_raw = const.tile([P, 512], BF16)
-        nc.vector.memset(gb_raw[:], 0.0)
-        nc.sync.dma_start(out=gb_raw[0:2, :], in_=g3.rearrange("(a i) -> a i", a=2))
-        nc.sync.dma_start(out=gb_raw[2:4, :], in_=be3.rearrange("(a i) -> a i", a=2))
-        load_ffh(0)
-        w2raw = const.tile([P, 4, D], BF16)
-        nc.sync.dma_start(out=w2raw[:], in_=w2.rearrange("(p j) c -> p j c", j=4))
         b2row = const.tile([P, D], BF16)
         nc.vector.memset(b2row[:], 0.0)
         nc.sync.dma_start(out=b2row[0:1, :], in_=b2.rearrange("(o d) -> o d", o=1))
         ones = const.tile([P, P], BF16)
         nc.vector.memset(ones[:], 1.0)
+        w2raw = const.tile([P, 4, D], BF16)
+
+        def load_w2(h):
+            nc.sync.dma_start(
+                out=w2raw[:, :, 512 * h : 512 * h + 512],
+                in_=w2[:, 512 * h : 512 * h + 512].rearrange("(p j) c -> p j c", j=4),
+            )
+
         load_tgt(0)
+        load_w2(0)
+        load_ffh(0)
+        load_w2(1)
+        gb_raw = const.tile([P, 512], BF16)
+        nc.vector.memset(gb_raw[:], 0.0)
+        nc.sync.dma_start(out=gb_raw[0:2, :], in_=g3.rearrange("(a i) -> a i", a=2))
+        nc.sync.dma_start(out=gb_raw[2:4, :], in_=be3.rearrange("(a i) -> a i", a=2))
         load_ffh(1)
         load_tgt(1)
         load_dup(0)
@@ -70,6 +83,9 @@ def tile_mldecoder_pb_t_kernel(tc, ff_hid, tgt, w2, b2, g3, be3, dup_pool, dup_b
         load_ffh(2)
         load_tgt(2)
         load_dup(2)
+        load_ffh(3)
+        load_tgt(3)
+        load_dup(3)
         dbias = const.tile([P, K * G], BF16)
 
         eps_t = const.tile([P, 1], F32)
@@ -85,14 +101,10 @@ def tile_mldecoder_pb_t_kernel(tc, ff_hid, tgt, w2, b2, g3, be3, dup_pool, dup_b
         w2s = const.tile([P, D], U8, align_bytes=64)
         w2g = const.tile([P, 2, 512, 4], BF16, align_bytes=64)
 
-        def regroup_w2():
-            nc.vector.tensor_copy(
-                out=w2g[:, 0].rearrange("p (t m) j -> p t m j", t=4),
-                in_=w2raw[:, :, 0:512].rearrange("p j (m t) -> p t m j", t=4),
-            )
-            nc.scalar.copy(
-                out=w2g[:, 1].rearrange("p (t m) j -> p t m j", t=4),
-                in_=w2raw[:, :, 512:1024].rearrange("p j (m t) -> p t m j", t=4),
+        def regroup_w2(copy, h, t0, t1):
+            copy(
+                out=w2g[:, h, P * t0 : P * t1].rearrange("p (t m) j -> p t m j", t=t1 - t0),
+                in_=w2raw[:, :, 512 * h : 512 * h + 512].rearrange("p j (m t) -> p t m j", t=4)[:, t0:t1],
             )
 
         def quant_w2(h):
@@ -151,34 +163,31 @@ def tile_mldecoder_pb_t_kernel(tc, ff_hid, tgt, w2, b2, g3, be3, dup_pool, dup_b
             )
             u_of[k] = u_t
 
-        def m1(k):
+        def m1(k, h):
             ffc, ffs = ff_q[k // 2]
             cols = slice(P * (k % 2), P * (k % 2) + P)
-            banks = []
-            for h in range(2):
-                s1 = psum.tile([P, 512], F32, tag="s1", bufs=2)
-                n_cols = slice(512 * h, 512 * h + 512)
-                nc.tensor.matmul_mx(
-                    out=s1[:],
-                    lhsT=ffc[:, cols].bitcast(FP8X4),
-                    lhsT_scale=ffs[:, cols],
-                    rhs=w2c[:, n_cols].bitcast(FP8X4),
-                    rhs_scale=w2s[:, n_cols],
-                    start=True,
-                    stop=True,
-                )
-                banks.append(s1)
-            s1_of[k] = banks
+            s1 = psum.tile([P, 512], F32, tag="s1", bufs=2)
+            n_cols = slice(512 * h, 512 * h + 512)
+            nc.tensor.matmul_mx(
+                out=s1[:],
+                lhsT=ffc[:, cols].bitcast(FP8X4),
+                lhsT_scale=ffs[:, cols],
+                rhs=w2c[:, n_cols].bitcast(FP8X4),
+                rhs_scale=w2s[:, n_cols],
+                start=True,
+                stop=True,
+            )
+            s1_of[k, h] = s1
 
-        def p1(k):
-            s0 = small.tile([P, 2], F32, tag="s0")
-            for h in range(2):
-                n_cols = slice(512 * h, 512 * h + 512)
-                nc.vector.scalar_tensor_tensor(
-                    out=u_of[k][:, n_cols], in0=s1_of[k][h][:], scalar=1.0, in1=u_of[k][:, n_cols],
-                    op0=ALU.mult, op1=ALU.add, accum_out=s0[:, h : h + 1],
-                )
-            s0_of[k] = s0
+        def p1(k, h):
+            if h == 0:
+                s0_new = small.tile([P, 2], F32, tag="s0")
+                s0_of[k] = s0_new
+            n_cols = slice(512 * h, 512 * h + 512)
+            nc.vector.scalar_tensor_tensor(
+                out=u_of[k][:, n_cols], in0=s1_of[k, h][:], scalar=1.0, in1=u_of[k][:, n_cols],
+                op0=ALU.mult, op1=ALU.add, accum_out=s0_of[k][:, h : h + 1],
+            )
 
         def nm(k):
             negm = small.tile([P, 1], F32, tag="negm")
@@ -236,18 +245,30 @@ def tile_mldecoder_pb_t_kernel(tc, ff_hid, tgt, w2, b2, g3, be3, dup_pool, dup_b
                 hp_of[k] = hp_new
             for t in range(4):
                 c = 4 * a + t
-                nc.scalar.activation(
-                    out=hp_of[k][:, c, :], in_=zT_of[k][a][:, t, :], func=ACT.Identity,
-                    bias=gb[:, t, 2 + a : 3 + a], scale=gb[:, t, a : a + 1],
-                )
+                if a == 1 and k >= AF_SHARED_FROM:
+                    nc.vector.tensor_scalar(
+                        out=hp_of[k][:, c, :], in0=zT_of[k][a][:, t, :],
+                        scalar1=gb[:, t, a : a + 1], scalar2=gb[:, t, 2 + a : 3 + a], op0=ALU.mult, op1=ALU.add,
+                    )
+                else:
+                    nc.scalar.activation(
+                        out=hp_of[k][:, c, :], in_=zT_of[k][a][:, t, :], func=ACT.Identity,
+                        bias=gb[:, t, 2 + a : 3 + a], scale=gb[:, t, a : a + 1],
+                    )
 
         def rg(k):
             hg = work.tile([P, 2, P, 4], BF16, tag="hg", bufs=3, align_bytes=64)
             nc.vector.tensor_copy(
-                out=hg[:].rearrange("p a (c i) t -> p a c t i", i=4),
-                in_=hp_of[k][:].rearrange("p (a t) (c i) -> p a c t i", t=4, i=4),
+                out=hg[:, 0].rearrange("p (c i) t -> p c t i", i=4),
+                in_=hp_of[k][:, 0:4, :].rearrange("p t (c i) -> p c t i", i=4),
             )
             hg_of[k] = hg
+
+        def rg_second(k):
+            nc.gpsimd.tensor_scalar(
+                out=hg_of[k][:, 1], in0=hp_of[k][:, 4:8, :].rearrange("p t b -> p b t"),
+                scalar1=1.0, scalar2=0.0, op0=ALU.mult, op1=ALU.add,
+            )
 
         def qh(k):
             hc = work.tile([P, 2 * P], U32, tag="hc", bufs=3, align_bytes=64)
@@ -278,16 +299,20 @@ def tile_mldecoder_pb_t_kernel(tc, ff_hid, tgt, w2, b2, g3, be3, dup_pool, dup_b
             )
             d_q[k] = (dc, ds)
 
+        def group_start(k):
+            return K - 1 if k == K - 1 else 4 * (k // 4)
+
         def m2(k):
-            if k % 4 == 0:
+            first = group_start(k)
+            if k == first:
                 o2_new = psum.tile([P, 4 * G], F32, tag="o2", bufs=2)
-                o2_t[k // 4] = o2_new
+                o2_t[first] = o2_new
             hc, hs = h_q[k]
             dc, ds = d_q[k]
             for a in range(2):
                 sl = slice(P * a, P * a + P)
                 nc.tensor.matmul_mx(
-                    out=o2_t[k // 4][:, G * (k % 4) : G * (k % 4) + G],
+                    out=o2_t[first][:, G * (k - first) : G * (k - first) + G],
                     lhsT=hc[:, sl].bitcast(FP8X4),
                     lhsT_scale=hs[:, sl],
                     rhs=dc[:, sl].bitcast(FP8X4),
@@ -296,35 +321,49 @@ def tile_mldecoder_pb_t_kernel(tc, ff_hid, tgt, w2, b2, g3, be3, dup_pool, dup_b
                     stop=(a == 1),
                 )
 
-        def oa(g):
-            o_cols = slice(4 * G * g, 4 * G * g + 4 * G)
+        def oa(k):
+            first = group_start(k)
+            width = G * (k - first + 1)
+            o_cols = slice(G * first, G * first + width)
             ob = work.tile([P, 4 * G], F32, tag="ob", bufs=2)
-            nc.vector.tensor_tensor(out=ob[:], in0=o2_t[g][:], in1=dbias[:, o_cols], op=ALU.add)
-            nc.sync.dma_start(out=out[:, o_cols], in_=ob[:])
+            nc.vector.tensor_tensor(out=ob[:, 0:width], in0=o2_t[first][:, 0:width], in1=dbias[:, o_cols], op=ALU.add)
+            nc.sync.dma_start(out=out[:, o_cols], in_=ob[:, 0:width])
 
         def tok(k):
             return 0 <= k < K
 
-        gain_shift_columns()
-        t_ff(0)
         spread_b2()
+        t_ff(0)
+        tb(0)
+        tb(1)
         c_ff(0)
-        q_ff(0)
-        regroup_w2()
+        regroup_w2(nc.vector.tensor_copy, 0, 0, 4)
+        regroup_w2(nc.scalar.copy, 1, 0, 3)
         quant_w2(0)
-        for n in range(-3, K + 8):
+        q_ff(0)
+        m1(0, 0)
+        t_ff(1)
+        c_ff(1)
+        regroup_w2(nc.vector.tensor_copy, 1, 3, 4)
+        p1(0, 0)
+        quant_w2(1)
+        m1(0, 1)
+        p1(0, 1)
+        gain_shift_columns()
+        for n in range(0, K + 8):
             if n % 2 == 0:
                 p_new = (n + 8) // 2
-                if 3 <= p_new < K // 2:
+                if p_new < K // 2:
                     load_ffh(p_new)
                     load_tgt(p_new)
                     load_dup(p_new)
             if n == 0:
                 nc.sync.dma_start(out=dbias[:], in_=dup_bias.partition_broadcast(P))
-            if tok(n):
-                p1(n)
-            if tok(n - 7) and (n - 7) % 4 == 3:
-                oa((n - 7) // 4)
+            if 0 < n < K:
+                p1(n, 0)
+                p1(n, 1)
+            if tok(n - 7) and (n - 7 == K - 1 or group_start(n - 6) != group_start(n - 7)):
+                oa(n - 7)
             if tok(n - 4):
                 af(n - 4, 0)
             if tok(n - 3):
@@ -332,22 +371,22 @@ def tile_mldecoder_pb_t_kernel(tc, ff_hid, tgt, w2, b2, g3, be3, dup_pool, dup_b
             if tok(n - 2):
                 sr(n - 2)
             if tok(n + 1):
-                m1(n + 1)
+                m1(n + 1, 0)
+                m1(n + 1, 1)
             if tok(n - 6):
                 m2(n - 6)
             if tok(n - 4):
                 af(n - 4, 1)
             if tok(n + 2):
                 tb(n + 2)
-            if n == -2:
-                quant_w2(1)
             if tok(n):
                 nm(n)
             if tok(n - 3):
                 tz(n - 3)
-            if n >= 0 and n % 2 == 0 and tok(n + 2):
+            if n % 2 == 0 and tok(n + 2):
                 q_ff((n + 2) // 2)
             if tok(n - 5):
+                rg_second(n - 5)
                 qh(n - 5)
             if tok(n - 4):
                 rg(n - 4)
@@ -359,7 +398,7 @@ def tile_mldecoder_pb_t_kernel(tc, ff_hid, tgt, w2, b2, g3, be3, dup_pool, dup_b
                 qd(n - 2)
             if tok(n):
                 dr(n)
-            if n >= -2 and n % 2 == 0 and tok(n + 4):
+            if n % 2 == 0 and tok(n + 4):
                 t_ff((n + 4) // 2)
-            if n >= -1 and (n + 3) % 2 == 0 and tok(n + 3):
+            if n % 2 == 1 and tok(n + 3):
                 c_ff((n + 3) // 2)

@@ -387,15 +387,16 @@ def tile_mldecoder_pb_t_kernel(tc, ff_hid, tgt, w2, b2, g3, be3, dup_pool, dup_b
                 q_ff((n + 2) // 2)
             if tok(n - 5):
                 rg_second(n - 5)
-                qh(n - 5)
             if tok(n - 4):
                 rg(n - 4)
+            if tok(n - 2):
+                qd(n - 2)
+            if tok(n - 5):
+                qh(n - 5)
             if tok(n - 1):
                 sq(n - 1)
             if tok(n - 2):
                 nbias(n - 2)
-            if tok(n - 2):
-                qd(n - 2)
             if tok(n):
                 dr(n)
             if n % 2 == 0 and tok(n + 4):

@@ -15,9 +15,7 @@ P = 128
 B, K, G, D, FF = 128, 32, 128, 1024, 512
 EPS = 1e-5
 FLOPS = 2 * B * K * FF * D + 2 * B * K * D * G
-DUP_ON_GPSIMD = True
-XH_ON_VECTOR_FROM = K - 3
-AF_SHARED_FROM = K - 4
+TAIL = K - 3
 AF_ON_VECTOR_EVERY = 64
 
 
@@ -218,8 +216,8 @@ def tile_mldecoder_pb_t_kernel(tc, ff_hid, tgt, w2, b2, g3, be3, dup_pool, dup_b
             nb_of[k] = nb
 
         def xh(k):
-            z = work.tile([P, D], F32, tag="z", bufs=2)
-            if k >= XH_ON_VECTOR_FROM:
+            z = work.tile([P, D], F32, tag="z", bufs=4)
+            if k >= TAIL:
                 nc.vector.tensor_scalar(
                     out=z[:], in0=u_of[k][:], scalar1=negm_of[k][:], scalar2=rstd_of[k][:], op0=ALU.add, op1=ALU.mult
                 )
@@ -232,7 +230,7 @@ def tile_mldecoder_pb_t_kernel(tc, ff_hid, tgt, w2, b2, g3, be3, dup_pool, dup_b
         def tz(k):
             banks = []
             for a in range(2):
-                zT = psum.tile([P, 4, P], F32, tag="zT", bufs=2)
+                zT = psum.tile([P, 4, P], F32, tag="s1" if k >= TAIL and k % 2 == 1 else "zT", bufs=2)
                 for t in range(4):
                     c = 4 * a + t
                     nc.tensor.transpose(zT[:, t, :], z_of[k][:, P * c : P * c + P], ident_f[:])
@@ -245,24 +243,33 @@ def tile_mldecoder_pb_t_kernel(tc, ff_hid, tgt, w2, b2, g3, be3, dup_pool, dup_b
                 hp_of[k] = hp_new
             for t in range(4):
                 c = 4 * a + t
-                if a == 1 and k >= AF_SHARED_FROM:
-                    nc.vector.tensor_scalar(
-                        out=hp_of[k][:, c, :], in0=zT_of[k][a][:, t, :],
-                        scalar1=gb[:, t, a : a + 1], scalar2=gb[:, t, 2 + a : 3 + a], op0=ALU.mult, op1=ALU.add,
-                    )
-                else:
-                    nc.scalar.activation(
-                        out=hp_of[k][:, c, :], in_=zT_of[k][a][:, t, :], func=ACT.Identity,
-                        bias=gb[:, t, 2 + a : 3 + a], scale=gb[:, t, a : a + 1],
-                    )
+                nc.scalar.activation(
+                    out=hp_of[k][:, c, :], in_=zT_of[k][a][:, t, :], func=ACT.Identity,
+                    bias=gb[:, t, 2 + a : 3 + a], scale=gb[:, t, a : a + 1],
+                )
+
+        def rg_half(copy, k, a):
+            copy(
+                out=hg_of[k][:, a].rearrange("p (c i) t -> p c t i", i=4),
+                in_=hp_of[k][:, 4 * a : 4 * a + 4, :].rearrange("p t (c i) -> p c t i", i=4),
+            )
 
         def rg(k):
             hg = work.tile([P, 2, P, 4], BF16, tag="hg", bufs=3, align_bytes=64)
-            nc.vector.tensor_copy(
-                out=hg[:, 0].rearrange("p (c i) t -> p c t i", i=4),
-                in_=hp_of[k][:, 0:4, :].rearrange("p t (c i) -> p c t i", i=4),
-            )
             hg_of[k] = hg
+            if rg_on_gpsimd(k):
+                rg_half(nc.vector.tensor_copy, k, 0)
+            elif k == K - 1:
+                rg_half(nc.vector.tensor_copy, k, 0)
+                rg_half(nc.scalar.copy, k, 1)
+            else:
+                nc.vector.tensor_copy(
+                    out=hg[:].rearrange("p a (c i) t -> p a c t i", i=4),
+                    in_=hp_of[k][:].rearrange("p (a t) (c i) -> p a c t i", t=4, i=4),
+                )
+
+        def rg_on_gpsimd(k):
+            return k < TAIL - 1
 
         def rg_second(k):
             nc.gpsimd.tensor_scalar(
@@ -280,7 +287,7 @@ def tile_mldecoder_pb_t_kernel(tc, ff_hid, tgt, w2, b2, g3, be3, dup_pool, dup_b
 
         def dr(k):
             dg = work.tile([P, 2, G, 4], BF16, tag="dg", bufs=2, align_bytes=64)
-            if DUP_ON_GPSIMD:
+            if k < K - 1:
                 nc.gpsimd.tensor_scalar(
                     out=dg[:], in0=dup_t[k // 2][:, k % 2].rearrange("p a (t g) -> p a g t", t=4),
                     scalar1=1.0, scalar2=0.0, op0=ALU.mult, op1=ALU.add,
@@ -350,7 +357,7 @@ def tile_mldecoder_pb_t_kernel(tc, ff_hid, tgt, w2, b2, g3, be3, dup_pool, dup_b
         m1(0, 1)
         p1(0, 1)
         gain_shift_columns()
-        for n in range(0, K + 8):
+        for n in range(0, K - 1):
             if n % 2 == 0:
                 p_new = (n + 8) // 2
                 if p_new < K // 2:
@@ -359,47 +366,91 @@ def tile_mldecoder_pb_t_kernel(tc, ff_hid, tgt, w2, b2, g3, be3, dup_pool, dup_b
                     load_dup(p_new)
             if n == 0:
                 nc.sync.dma_start(out=dbias[:], in_=dup_bias.partition_broadcast(P))
-            if 0 < n < K:
+            if n > 0:
                 p1(n, 0)
                 p1(n, 1)
-            if tok(n - 7) and (n - 7 == K - 1 or group_start(n - 6) != group_start(n - 7)):
-                oa(n - 7)
-            if tok(n - 4):
-                af(n - 4, 0)
-            if tok(n - 3):
-                xh(n - 3)
-            if tok(n - 2):
-                sr(n - 2)
-            if tok(n + 1):
-                m1(n + 1, 0)
-                m1(n + 1, 1)
-            if tok(n - 6):
-                m2(n - 6)
-            if tok(n - 4):
-                af(n - 4, 1)
-            if tok(n + 2):
-                tb(n + 2)
-            if tok(n):
-                nm(n)
-            if tok(n - 3):
-                tz(n - 3)
-            if n % 2 == 0 and tok(n + 2):
-                q_ff((n + 2) // 2)
-            if tok(n - 5):
-                rg_second(n - 5)
-            if tok(n - 4):
-                rg(n - 4)
-            if tok(n - 2):
-                qd(n - 2)
-            if tok(n - 5):
-                qh(n - 5)
+            if tok(n - 6) and group_start(n - 5) != group_start(n - 6):
+                oa(n - 6)
+            if n == 0:
+                nm(0)
             if tok(n - 1):
                 sq(n - 1)
+            if tok(n - 3):
+                af(n - 3, 0)
+            m1(n + 1, 0)
+            m1(n + 1, 1)
+            if tok(n - 5):
+                m2(n - 5)
+            if tok(n + 2):
+                tb(n + 2)
+            if n > 0:
+                nm(n)
             if tok(n - 2):
-                nbias(n - 2)
-            if tok(n):
-                dr(n)
-            if n % 2 == 0 and tok(n + 4):
-                t_ff((n + 4) // 2)
+                xh(n - 2)
+            if tok(n - 1):
+                sr(n - 1)
+            if tok(n - 3):
+                af(n - 3, 1)
+            if tok(n - 1) and n - 1 < TAIL:
+                nbias(n - 1)
             if n % 2 == 1 and tok(n + 3):
                 c_ff((n + 3) // 2)
+            if tok(n - 2):
+                tz(n - 2)
+            if n % 2 == 0 and tok(n + 4):
+                t_ff((n + 4) // 2)
+            if n % 2 == 0 and tok(n + 2):
+                q_ff((n + 2) // 2)
+            if tok(n - 4):
+                rg_second(n - 4)
+            if tok(n - 3):
+                rg(n - 3)
+            if tok(n - 2):
+                qd(n - 2)
+            if tok(n - 4):
+                qh(n - 4)
+            dr(n)
+        p1(31, 0)
+        p1(31, 1)
+        sq(30)
+        rg_second(27)
+        m2(26)
+        xh(29)
+        af(28, 0)
+        af(28, 1)
+        tz(29)
+        nm(31)
+        sr(30)
+        qd(29)
+        qh(27)
+        m2(27)
+        sq(31)
+        xh(30)
+        tz(30)
+        rg(28)
+        af(29, 0)
+        sr(31)
+        af(29, 1)
+        qh(28)
+        m2(28)
+        xh(31)
+        tz(31)
+        rg(29)
+        oa(27)
+        af(30, 0)
+        af(30, 1)
+        qh(29)
+        m2(29)
+        qd(30)
+        dr(31)
+        rg(30)
+        qd(31)
+        qh(30)
+        m2(30)
+        af(31, 0)
+        af(31, 1)
+        oa(30)
+        rg(31)
+        qh(31)
+        m2(31)
+        oa(31)

@@ -55,27 +55,26 @@ def tile_mldecoder_pb_t_kernel(tc, ff_hid, tgt, w2, b2, g3, be3, dup_pool, dup_b
 
         b2row = const.tile([P, D], BF16)
         nc.vector.memset(b2row[:], 0.0)
-        nc.sync.dma_start(out=b2row[0:1, :], in_=b2.rearrange("(o d) -> o d", o=1))
         ones = const.tile([P, P], BF16)
         nc.vector.memset(ones[:], 1.0)
-        w2raw = const.tile([P, 4, D], BF16)
+        w2raw = {}
 
         def load_w2(h):
-            nc.sync.dma_start(
-                out=w2raw[:, :, 512 * h : 512 * h + 512],
-                in_=w2[:, 512 * h : 512 * h + 512].rearrange("(p j) c -> p j c", j=4),
-            )
+            raw = const.tile([P, 4, 512], BF16, tag=f"w2raw{h}")
+            nc.sync.dma_start(out=raw[:], in_=w2[:, 512 * h : 512 * h + 512].rearrange("(p j) c -> p j c", j=4))
+            w2raw[h] = raw
 
-        load_tgt(0)
         load_w2(0)
+        nc.sync.dma_start(out=b2row[0:1, :], in_=b2.rearrange("(o d) -> o d", o=1))
         load_ffh(0)
+        load_tgt(0)
         load_w2(1)
+        load_ffh(1)
+        load_tgt(1)
         gb_raw = const.tile([P, 512], BF16)
         nc.vector.memset(gb_raw[:], 0.0)
         nc.sync.dma_start(out=gb_raw[0:2, :], in_=g3.rearrange("(a i) -> a i", a=2))
         nc.sync.dma_start(out=gb_raw[2:4, :], in_=be3.rearrange("(a i) -> a i", a=2))
-        load_ffh(1)
-        load_tgt(1)
         load_dup(0)
         load_dup(1)
         load_ffh(2)
@@ -102,7 +101,7 @@ def tile_mldecoder_pb_t_kernel(tc, ff_hid, tgt, w2, b2, g3, be3, dup_pool, dup_b
         def regroup_w2(copy, h, t0, t1):
             copy(
                 out=w2g[:, h, P * t0 : P * t1].rearrange("p (t m) j -> p t m j", t=t1 - t0),
-                in_=w2raw[:, :, 512 * h : 512 * h + 512].rearrange("p j (m t) -> p t m j", t=4)[:, t0:t1],
+                in_=w2raw[h][:].rearrange("p j (m t) -> p t m j", t=4)[:, t0:t1],
             )
 
         def quant_w2(h):
@@ -339,24 +338,25 @@ def tile_mldecoder_pb_t_kernel(tc, ff_hid, tgt, w2, b2, g3, be3, dup_pool, dup_b
         def tok(k):
             return 0 <= k < K
 
+        regroup_w2(nc.vector.tensor_copy, 0, 0, 2)
+        regroup_w2(nc.scalar.copy, 0, 2, 4)
+        quant_w2(0)
         spread_b2()
         t_ff(0)
-        tb(0)
-        tb(1)
         c_ff(0)
-        regroup_w2(nc.vector.tensor_copy, 0, 0, 4)
-        regroup_w2(nc.scalar.copy, 1, 0, 3)
-        quant_w2(0)
+        tb(0)
         q_ff(0)
         m1(0, 0)
         t_ff(1)
-        c_ff(1)
+        tb(1)
+        regroup_w2(nc.scalar.copy, 1, 0, 3)
         regroup_w2(nc.vector.tensor_copy, 1, 3, 4)
+        c_ff(1)
         p1(0, 0)
         quant_w2(1)
         m1(0, 1)
+        tb(2)
         p1(0, 1)
-        gain_shift_columns()
         for n in range(0, K - 1):
             if n % 2 == 0:
                 p_new = (n + 8) // 2
@@ -381,10 +381,12 @@ def tile_mldecoder_pb_t_kernel(tc, ff_hid, tgt, w2, b2, g3, be3, dup_pool, dup_b
             m1(n + 1, 1)
             if tok(n - 5):
                 m2(n - 5)
-            if tok(n + 2):
+            if n > 0 and tok(n + 2):
                 tb(n + 2)
             if n > 0:
                 nm(n)
+            if n == 1:
+                gain_shift_columns()
             if tok(n - 2):
                 xh(n - 2)
             if tok(n - 1):

@@ -15,7 +15,7 @@ P = 128
 B, K, G, D, FF = 128, 32, 128, 1024, 512
 EPS = 1e-5
 FLOPS = 2 * B * K * FF * D + 2 * B * K * D * G
-TAIL = K - 3
+TAIL = K - 4
 AF_ON_VECTOR_EVERY = 64
 
 
@@ -247,14 +247,37 @@ def tile_mldecoder_pb_t_kernel(tc, ff_hid, tgt, w2, b2, g3, be3, dup_pool, dup_b
                     bias=gb[:, t, 2 + a : 3 + a], scale=gb[:, t, a : a + 1],
                 )
 
+        def tz_pair(p, i):
+            zT = psum.tile([P, 2, 2, P], F32, tag="zT", bufs=2)
+            for e in range(2):
+                c = 2 * i + e
+                for j in range(2):
+                    nc.tensor.transpose(zT[:, e, j, :], z_of[2 * p + j][:, P * c : P * c + P], ident_f[:])
+            zT_of["pair", p, i] = zT
+
+        def af_pair(p, i):
+            if i == 0:
+                hp_new = work.tile([P, 2, 8, P], BF16, tag="hp_pair", bufs=2)
+                hp_of["pair", p] = hp_new
+            for e in range(2):
+                c = 2 * i + e
+                a, t = c // 4, c % 4
+                nc.scalar.activation(
+                    out=hp_of["pair", p][:, :, c, :], in_=zT_of["pair", p, i][:, e], func=ACT.Identity,
+                    bias=gb[:, t, 2 + a : 3 + a], scale=gb[:, t, a : a + 1],
+                )
+
+        def hp_rows(k, c0, c1):
+            return hp_of["pair", k // 2][:, k % 2, c0:c1, :] if k < TAIL else hp_of[k][:, c0:c1, :]
+
         def rg_half(copy, k, a):
             copy(
                 out=hg_of[k][:, a].rearrange("p (c i) t -> p c t i", i=4),
-                in_=hp_of[k][:, 4 * a : 4 * a + 4, :].rearrange("p t (c i) -> p c t i", i=4),
+                in_=hp_rows(k, 4 * a, 4 * a + 4).rearrange("p t (c i) -> p c t i", i=4),
             )
 
         def rg(k):
-            hg = work.tile([P, 2, P, 4], BF16, tag="hg", bufs=3, align_bytes=64)
+            hg = work.tile([P, 2, P, 4], BF16, tag="hg", bufs=4, align_bytes=64)
             hg_of[k] = hg
             if rg_on_gpsimd(k):
                 rg_half(nc.vector.tensor_copy, k, 0)
@@ -264,15 +287,15 @@ def tile_mldecoder_pb_t_kernel(tc, ff_hid, tgt, w2, b2, g3, be3, dup_pool, dup_b
             else:
                 nc.vector.tensor_copy(
                     out=hg[:].rearrange("p a (c i) t -> p a c t i", i=4),
-                    in_=hp_of[k][:].rearrange("p (a t) (c i) -> p a c t i", t=4, i=4),
+                    in_=hp_rows(k, 0, 8).rearrange("p (a t) (c i) -> p a c t i", t=4, i=4),
                 )
 
         def rg_on_gpsimd(k):
-            return k < TAIL - 1
+            return k < TAIL
 
         def rg_second(k):
             nc.gpsimd.tensor_scalar(
-                out=hg_of[k][:, 1], in0=hp_of[k][:, 4:8, :].rearrange("p t b -> p b t"),
+                out=hg_of[k][:, 1], in0=hp_rows(k, 4, 8).rearrange("p t b -> p b t"),
                 scalar1=1.0, scalar2=0.0, op0=ALU.mult, op1=ALU.add,
             )
 
@@ -298,8 +321,8 @@ def tile_mldecoder_pb_t_kernel(tc, ff_hid, tgt, w2, b2, g3, be3, dup_pool, dup_b
             dg_of[k] = dg
 
         def qd(k):
-            dc = work.tile([P, 2 * G], U32, tag="dc", bufs=6, align_bytes=64)
-            ds = work.tile([P, 2 * G], U8, tag="ds", bufs=6, align_bytes=64)
+            dc = work.tile([P, 2 * G], U32, tag="dc", bufs=8, align_bytes=64)
+            ds = work.tile([P, 2 * G], U8, tag="ds", bufs=8, align_bytes=64)
             nc.vector.quantize_mx(
                 out=dc[:].bitcast(FP8X4), scales=ds[:], in_=dg_of[k][:].rearrange("p a g t -> p (a g t)")
             )
@@ -369,18 +392,19 @@ def tile_mldecoder_pb_t_kernel(tc, ff_hid, tgt, w2, b2, g3, be3, dup_pool, dup_b
             if n > 0:
                 p1(n, 0)
                 p1(n, 1)
-            if tok(n - 6) and group_start(n - 5) != group_start(n - 6):
-                oa(n - 6)
+            if tok(n - 8) and group_start(n - 7) != group_start(n - 8):
+                oa(n - 8)
             if n == 0:
                 nm(0)
             if tok(n - 1):
                 sq(n - 1)
-            if tok(n - 3):
-                af(n - 3, 0)
+            p_af, i_af = (n - 4) // 2, 2 * (n % 2)
+            if p_af >= 0:
+                af_pair(p_af, i_af)
             m1(n + 1, 0)
             m1(n + 1, 1)
-            if tok(n - 5):
-                m2(n - 5)
+            if tok(n - 7):
+                m2(n - 7)
             if n > 0 and tok(n + 2):
                 tb(n + 2)
             if n > 0:
@@ -391,52 +415,68 @@ def tile_mldecoder_pb_t_kernel(tc, ff_hid, tgt, w2, b2, g3, be3, dup_pool, dup_b
                 xh(n - 2)
             if tok(n - 1):
                 sr(n - 1)
-            if tok(n - 3):
-                af(n - 3, 1)
+            if p_af >= 0:
+                af_pair(p_af, i_af + 1)
             if tok(n - 1) and n - 1 < TAIL:
                 nbias(n - 1)
             if n % 2 == 1 and tok(n + 3):
                 c_ff((n + 3) // 2)
-            if tok(n - 2):
-                tz(n - 2)
+            if n % 2 == 0 and n >= 4:
+                tz_pair((n - 4) // 2, 2)
+                tz_pair((n - 4) // 2, 3)
+            if n % 2 == 1 and n >= 3:
+                tz_pair((n - 3) // 2, 0)
+                tz_pair((n - 3) // 2, 1)
             if n % 2 == 0 and tok(n + 4):
                 t_ff((n + 4) // 2)
             if n % 2 == 0 and tok(n + 2):
                 q_ff((n + 2) // 2)
-            if tok(n - 4):
-                rg_second(n - 4)
-            if tok(n - 3):
-                rg(n - 3)
+            if tok(n - 6):
+                rg_second(n - 6)
+            if tok(n - 5):
+                rg(n - 5)
             if tok(n - 2):
                 qd(n - 2)
-            if tok(n - 4):
-                qh(n - 4)
+            if tok(n - 6):
+                qh(n - 6)
             dr(n)
         p1(31, 0)
         p1(31, 1)
         sq(30)
-        rg_second(27)
-        m2(26)
+        af_pair(13, 2)
+        rg_second(25)
+        m2(24)
         xh(29)
-        af(28, 0)
-        af(28, 1)
-        tz(29)
+        af_pair(13, 3)
+        tz(28)
         nm(31)
         sr(30)
+        oa(23)
         qd(29)
-        qh(27)
-        m2(27)
+        rg(26)
+        qh(25)
+        m2(25)
+        rg_second(26)
+        rg(27)
+        rg_second(27)
         sq(31)
         xh(30)
+        tz(29)
+        af(28, 0)
+        sr(31)
+        af(28, 1)
+        qh(26)
+        m2(26)
+        xh(31)
         tz(30)
         rg(28)
         af(29, 0)
-        sr(31)
         af(29, 1)
+        tz(31)
+        qh(27)
+        m2(27)
         qh(28)
         m2(28)
-        xh(31)
-        tz(31)
         rg(29)
         oa(27)
         af(30, 0)

@@ -214,9 +214,12 @@ def tile_mldecoder_pb_t_kernel(tc, ff_hid, tgt, w2, b2, g3, be3, dup_pool, dup_b
             nc.scalar.activation(out=nb[:], in_=negm_of[k][:], func=ACT.Copy, scale=rstd_of[k][:])
             nb_of[k] = nb
 
+        def xh_on_vector(k):
+            return k >= TAIL or k % 8 == 6
+
         def xh(k):
             z = work.tile([P, D], F32, tag="z", bufs=4)
-            if k >= TAIL:
+            if xh_on_vector(k):
                 nc.vector.tensor_scalar(
                     out=z[:], in0=u_of[k][:], scalar1=negm_of[k][:], scalar2=rstd_of[k][:], op0=ALU.add, op1=ALU.mult
                 )
@@ -417,7 +420,7 @@ def tile_mldecoder_pb_t_kernel(tc, ff_hid, tgt, w2, b2, g3, be3, dup_pool, dup_b
                 sr(n - 1)
             if p_af >= 0:
                 af_pair(p_af, i_af + 1)
-            if tok(n - 1) and n - 1 < TAIL:
+            if tok(n - 1) and not xh_on_vector(n - 1):
                 nbias(n - 1)
             if n % 2 == 1 and tok(n + 3):
                 c_ff((n + 3) // 2)
@@ -477,22 +480,22 @@ def tile_mldecoder_pb_t_kernel(tc, ff_hid, tgt, w2, b2, g3, be3, dup_pool, dup_b
         m2(27)
         qh(28)
         m2(28)
+        qd(30)
         rg(29)
-        oa(27)
-        af(30, 0)
-        af(30, 1)
+        dr(31)
         qh(29)
         m2(29)
-        qd(30)
-        dr(31)
+        af(30, 0)
+        af(30, 1)
+        oa(27)
         rg(30)
         qd(31)
         qh(30)
         m2(30)
         af(31, 0)
         af(31, 1)
-        oa(30)
         rg(31)
         qh(31)
         m2(31)
+        oa(30)
         oa(31)

from contextlib import ExitStack

import concourse.mybir as mybir
from concourse.masks import make_identity

F32 = mybir.dt.float32
BF16 = mybir.dt.bfloat16
U32 = mybir.dt.uint32
U8 = mybir.dt.uint8
FP8X4 = mybir.dt.float8_e4m3fn_x4
ALU = mybir.AluOpType
ACT = mybir.ActivationFunctionType

P = 128
B, K, G, D, FF = 128, 32, 128, 1024, 512
EPS = 1e-5
FLOPS = 2 * B * K * FF * D + 2 * B * K * D * G
TAIL = K - 4
AF_ON_VECTOR_EVERY = 64


def tile_mldecoder_pb_t_kernel(tc, ff_hid, tgt, w2, b2, g3, be3, dup_pool, dup_bias, out):
    nc = tc.nc
    with ExitStack() as ctx:
        const = ctx.enter_context(tc.tile_pool(name="const", bufs=1))
        loads = ctx.enter_context(tc.tile_pool(name="loads", bufs=5))
        work = ctx.enter_context(tc.tile_pool(name="work", bufs=2))
        small = ctx.enter_context(tc.tile_pool(name="small", bufs=8))
        psum = ctx.enter_context(tc.psum_pool(name="psum", bufs=2))
        ctx.enter_context(tc.manual_schedule())

        ffh_t, tgt_t, dup_t = {}, {}, {}
        ffT_t, ffg_t, ff_q = {}, {}, {}
        u_of, s1_of, s0_of, negm_of, ss_of, std_of, rstd_of, nb_of = {}, {}, {}, {}, {}, {}, {}, {}
        z_of, zT_of, hp_of, hg_of, h_q, dg_of, d_q, o2_t = {}, {}, {}, {}, {}, {}, {}, {}

        def load_ffh(p):
            ffh = loads.tile([P, 2, FF], BF16, tag="ffh", bufs=4)
            nc.sync.dma_start(out=ffh[:], in_=ff_hid[:, 2 * p : 2 * p + 2, :])
            ffh_t[p] = ffh

        def load_tgt(p):
            tg = loads.tile([P, 2, D], BF16, tag="tg", bufs=5)
            if p == 0:
                for j in range(2):
                    nc.sync.dma_start(out=tg[:, j, :], in_=tgt[:, j, :])
            else:
                nc.sync.dma_start(out=tg[:], in_=tgt[:, 2 * p : 2 * p + 2, :])
            tgt_t[p] = tg

        def load_dup(p):
            dr_t = loads.tile([P, 2, 2, 4 * G], BF16, tag="dr", bufs=5)
            nc.sync.dma_start(out=dr_t[:], in_=dup_pool[2 * p : 2 * p + 2].rearrange("k (a p t) g -> p k a (t g)", p=P, t=4))
            dup_t[p] = dr_t

        b2row = const.tile([P, D], BF16)
        nc.vector.memset(b2row[:], 0.0)
        ones = const.tile([P, P], BF16)
        nc.vector.memset(ones[:], 1.0)
        w2raw = {}

        def load_w2(h):
            raw = const.tile([P, 4, 512], BF16, tag=f"w2raw{h}")
            nc.sync.dma_start(out=raw[:], in_=w2[:, 512 * h : 512 * h + 512].rearrange("(p j) c -> p j c", j=4))
            w2raw[h] = raw

        load_w2(0)
        nc.sync.dma_start(out=b2row[0:1, :], in_=b2.rearrange("(o d) -> o d", o=1))
        load_ffh(0)
        load_tgt(0)
        load_w2(1)
        load_ffh(1)
        load_tgt(1)
        gb_raw = const.tile([P, 512], BF16)
        nc.vector.memset(gb_raw[:], 0.0)
        nc.sync.dma_start(out=gb_raw[0:2, :], in_=g3.rearrange("(a i) -> a i", a=2))
        nc.sync.dma_start(out=gb_raw[2:4, :], in_=be3.rearrange("(a i) -> a i", a=2))
        load_dup(0)
        load_dup(1)
        load_ffh(2)
        load_tgt(2)
        load_dup(2)
        load_ffh(3)
        load_tgt(3)
        load_dup(3)
        dbias = const.tile([P, K * G], BF16)

        eps_t = const.tile([P, 1], F32)
        nc.vector.memset(eps_t[:], EPS)
        warm = const.tile([P, 1], F32)
        nc.scalar.activation(out=warm[:], in_=eps_t[:], func=ACT.Abs_reciprocal_sqrt)
        ident_f = const.tile([P, P], F32)
        make_identity(nc, ident_f[:])
        ident_b = const.tile([P, P], BF16)
        make_identity(nc, ident_b[:])

        w2c = const.tile([P, D], U32, align_bytes=64)
        w2s = const.tile([P, D], U8, align_bytes=64)
        w2g = const.tile([P, 2, 512, 4], BF16, align_bytes=64)

        def regroup_w2(copy, h, t0, t1):
            copy(
                out=w2g[:, h, P * t0 : P * t1].rearrange("p (t m) j -> p t m j", t=t1 - t0),
                in_=w2raw[h][:].rearrange("p j (m t) -> p t m j", t=4)[:, t0:t1],
            )

        def quant_w2(h):
            nc.vector.quantize_mx(
                out=w2c[:, 512 * h : 512 * h + 512].bitcast(FP8X4),
                scales=w2s[:, 512 * h : 512 * h + 512],
                in_=w2g[:, h].rearrange("p c t -> p (c t)"),
            )

        gb = const.tile([P, 4, 4], F32)

        def gain_shift_columns():
            gb_ps = psum.tile([P, 4, P], BF16, tag="o2", bufs=2)
            for t in range(4):
                nc.tensor.transpose(gb_ps[:, t, :], gb_raw[:, t:512:4], ident_b[:])
            nc.vector.tensor_copy(out=gb[:], in_=gb_ps[:, :, 0:4])

        b2bc = psum.tile([P, 2, 4, P], BF16, tag="b2", bufs=1)

        def spread_b2():
            for a in range(2):
                for t in range(4):
                    nc.tensor.matmul(
                        b2bc[:, a, t, :], lhsT=ones[:], rhs=b2row[:, 512 * a + t : 512 * a + 512 : 4], start=True, stop=True
                    )

        def t_ff(p):
            ffT = psum.tile([P, 2, 2, P], F32, tag="ffT", bufs=1)
            for j in range(2):
                k = 2 * p + j
                words = ffh_t[p][:, j, :].bitcast(F32)
                for u in range(2):
                    nc.tensor.transpose(ffT[:, j, u, :], words[:, u : 2 * P : 2], ident_f[:])
            ffT_t[p] = ffT

        def c_ff(p):
            ffg = work.tile([P, 2, P, 4], BF16, tag="ffg", bufs=2, align_bytes=64)
            nc.scalar.copy(out=ffg[:].bitcast(F32), in_=ffT_t[p][:].rearrange("p j u b -> p j b u"))
            ffg_t[p] = ffg

        def q_ff(p):
            ffc = work.tile([P, 2 * P], U32, tag="ffc", bufs=3, align_bytes=64)
            ffs = work.tile([P, 2 * P], U8, tag="ffs", bufs=3, align_bytes=64)
            nc.vector.quantize_mx(
                out=ffc[:].bitcast(FP8X4), scales=ffs[:], in_=ffg_t[p][:].rearrange("p j b t -> p (j b t)")
            )
            ff_q[p] = (ffc, ffs)

        def tb(k):
            u_t = work.tile([P, D], F32, tag="u", bufs=7)
            nc.vector.tensor_tensor(
                out=u_t[:].rearrange("p (a t m) -> p a t m", a=2, t=4),
                in0=b2bc[:],
                in1=tgt_t[k // 2][:, k % 2, :].rearrange("p (a m t) -> p a t m", a=2, t=4),
                op=ALU.add,
            )
            u_of[k] = u_t

        def m1(k, h):
            ffc, ffs = ff_q[k // 2]
            cols = slice(P * (k % 2), P * (k % 2) + P)
            s1 = psum.tile([P, 512], F32, tag="s1", bufs=2)
            n_cols = slice(512 * h, 512 * h + 512)
            nc.tensor.matmul_mx(
                out=s1[:],
                lhsT=ffc[:, cols].bitcast(FP8X4),
                lhsT_scale=ffs[:, cols],
                rhs=w2c[:, n_cols].bitcast(FP8X4),
                rhs_scale=w2s[:, n_cols],
                start=True,
                stop=True,
            )
            s1_of[k, h] = s1

        def p1(k, h):
            if h == 0:
                s0_new = small.tile([P, 2], F32, tag="s0")
                s0_of[k] = s0_new
            n_cols = slice(512 * h, 512 * h + 512)
            nc.vector.scalar_tensor_tensor(
                out=u_of[k][:, n_cols], in0=s1_of[k, h][:], scalar=1.0, in1=u_of[k][:, n_cols],
                op0=ALU.mult, op1=ALU.add, accum_out=s0_of[k][:, h : h + 1],
            )

        def nm(k):
            negm = small.tile([P, 1], F32, tag="negm")
            s0 = s0_of[k]
            nc.vector.tensor_scalar(
                out=negm[:], in0=s0[:, 0:1], scalar1=s0[:, 1:2], scalar2=-1.0 / D, op0=ALU.add, op1=ALU.mult
            )
            negm_of[k] = negm

        def sq(k):
            junk = work.tile([P, D], BF16, tag="junk", bufs=1)
            ss = small.tile([P, 1], F32, tag="ss")
            nc.scalar.activation(
                out=junk[:], in_=u_of[k][:], func=ACT.Square, bias=negm_of[k][:], scale=1.0, accum_out=ss[:]
            )
            ss_of[k] = ss

        def sr(k):
            rstd = small.tile([P, 1], F32, tag="rstd")
            nc.scalar.activation(
                out=rstd[:], in_=ss_of[k][:], func=ACT.Abs_reciprocal_sqrt, bias=eps_t[:], scale=1.0 / D
            )
            rstd_of[k] = rstd

        def nbias(k):
            nb = small.tile([P, 1], F32, tag="nb")
            nc.scalar.activation(out=nb[:], in_=negm_of[k][:], func=ACT.Copy, scale=rstd_of[k][:])
            nb_of[k] = nb

        def xh_on_vector(k):
            return k >= TAIL or k % 8 == 6

        def xh(k):
            z = work.tile([P, D], F32, tag="z", bufs=4)
            if xh_on_vector(k):
                nc.vector.tensor_scalar(
                    out=z[:], in0=u_of[k][:], scalar1=negm_of[k][:], scalar2=rstd_of[k][:], op0=ALU.add, op1=ALU.mult
                )
            else:
                nc.scalar.activation(
                    out=z[:], in_=u_of[k][:], func=ACT.Identity, bias=nb_of[k][:], scale=rstd_of[k][:]
                )
            z_of[k] = z

        def tz(k):
            banks = []
            for a in range(2):
                zT = psum.tile([P, 4, P], F32, tag="s1" if k >= TAIL and k % 2 == 1 else "zT", bufs=2)
                for t in range(4):
                    c = 4 * a + t
                    nc.tensor.transpose(zT[:, t, :], z_of[k][:, P * c : P * c + P], ident_f[:])
                banks.append(zT)
            zT_of[k] = banks

        def af(k, a):
            if a == 0:
                hp_new = work.tile([P, 8, P], BF16, tag="hp", bufs=2)
                hp_of[k] = hp_new
            for t in range(4):
                c = 4 * a + t
                nc.scalar.activation(
                    out=hp_of[k][:, c, :], in_=zT_of[k][a][:, t, :], func=ACT.Identity,
                    bias=gb[:, t, 2 + a : 3 + a], scale=gb[:, t, a : a + 1],
                )

        def tz_pair(p, i):
            zT = psum.tile([P, 2, 2, P], F32, tag="zT", bufs=2)
            for e in range(2):
                c = 2 * i + e
                for j in range(2):
                    nc.tensor.transpose(zT[:, e, j, :], z_of[2 * p + j][:, P * c : P * c + P], ident_f[:])
            zT_of["pair", p, i] = zT

        def af_pair(p, i):
            if i == 0:
                hp_new = work.tile([P, 2, 8, P], BF16, tag="hp_pair", bufs=2)
                hp_of["pair", p] = hp_new
            for e in range(2):
                c = 2 * i + e
                a, t = c // 4, c % 4
                nc.scalar.activation(
                    out=hp_of["pair", p][:, :, c, :], in_=zT_of["pair", p, i][:, e], func=ACT.Identity,
                    bias=gb[:, t, 2 + a : 3 + a], scale=gb[:, t, a : a + 1],
                )

        def hp_rows(k, c0, c1):
            return hp_of["pair", k // 2][:, k % 2, c0:c1, :] if k < TAIL else hp_of[k][:, c0:c1, :]

        def rg_half(copy, k, a):
            copy(
                out=hg_of[k][:, a].rearrange("p (c i) t -> p c t i", i=4),
                in_=hp_rows(k, 4 * a, 4 * a + 4).rearrange("p t (c i) -> p c t i", i=4),
            )

        def rg(k):
            hg = work.tile([P, 2, P, 4], BF16, tag="hg", bufs=4, align_bytes=64)
            hg_of[k] = hg
            if rg_on_gpsimd(k):
                rg_half(nc.vector.tensor_copy, k, 0)
            elif k == K - 1:
                rg_half(nc.vector.tensor_copy, k, 0)
                rg_half(nc.scalar.copy, k, 1)
            else:
                nc.vector.tensor_copy(
                    out=hg[:].rearrange("p a (c i) t -> p a c t i", i=4),
                    in_=hp_rows(k, 0, 8).rearrange("p (a t) (c i) -> p a c t i", t=4, i=4),
                )

        def rg_on_gpsimd(k):
            return k < TAIL

        def rg_second(k):
            nc.gpsimd.tensor_scalar(
                out=hg_of[k][:, 1], in0=hp_rows(k, 4, 8).rearrange("p t b -> p b t"),
                scalar1=1.0, scalar2=0.0, op0=ALU.mult, op1=ALU.add,
            )

        def qh(k):
            hc = work.tile([P, 2 * P], U32, tag="hc", bufs=3, align_bytes=64)
            hs = work.tile([P, 2 * P], U8, tag="hs", bufs=3, align_bytes=64)
            nc.vector.quantize_mx(
                out=hc[:].bitcast(FP8X4), scales=hs[:], in_=hg_of[k][:].rearrange("p a b t -> p (a b t)")
            )
            h_q[k] = (hc, hs)

        def dr(k):
            dg = work.tile([P, 2, G, 4], BF16, tag="dg", bufs=2, align_bytes=64)
            if k < K - 1:
                nc.gpsimd.tensor_scalar(
                    out=dg[:], in0=dup_t[k // 2][:, k % 2].rearrange("p a (t g) -> p a g t", t=4),
                    scalar1=1.0, scalar2=0.0, op0=ALU.mult, op1=ALU.add,
                )
            else:
                nc.vector.tensor_copy(
                    out=dg[:], in_=dup_t[k // 2][:, k % 2].rearrange("p a (t g) -> p a g t", t=4)
                )
            dg_of[k] = dg

        def qd(k):
            dc = work.tile([P, 2 * G], U32, tag="dc", bufs=8, align_bytes=64)
            ds = work.tile([P, 2 * G], U8, tag="ds", bufs=8, align_bytes=64)
            nc.vector.quantize_mx(
                out=dc[:].bitcast(FP8X4), scales=ds[:], in_=dg_of[k][:].rearrange("p a g t -> p (a g t)")
            )
            d_q[k] = (dc, ds)

        def group_start(k):
            return K - 1 if k == K - 1 else 4 * (k // 4)

        def m2(k):
            first = group_start(k)
            if k == first:
                o2_new = psum.tile([P, 4 * G], F32, tag="o2", bufs=2)
                o2_t[first] = o2_new
            hc, hs = h_q[k]
            dc, ds = d_q[k]
            for a in range(2):
                sl = slice(P * a, P * a + P)
                nc.tensor.matmul_mx(
                    out=o2_t[first][:, G * (k - first) : G * (k - first) + G],
                    lhsT=hc[:, sl].bitcast(FP8X4),
                    lhsT_scale=hs[:, sl],
                    rhs=dc[:, sl].bitcast(FP8X4),
                    rhs_scale=ds[:, sl],
                    start=(a == 0),
                    stop=(a == 1),
                )

        def oa(k):
            first = group_start(k)
            width = G * (k - first + 1)
            o_cols = slice(G * first, G * first + width)
            ob = work.tile([P, 4 * G], F32, tag="ob", bufs=2)
            nc.vector.tensor_tensor(out=ob[:, 0:width], in0=o2_t[first][:, 0:width], in1=dbias[:, o_cols], op=ALU.add)
            nc.sync.dma_start(out=out[:, o_cols], in_=ob[:, 0:width])

        def tok(k):
            return 0 <= k < K

        regroup_w2(nc.vector.tensor_copy, 0, 0, 2)
        regroup_w2(nc.scalar.copy, 0, 2, 4)
        quant_w2(0)
        spread_b2()
        t_ff(0)
        c_ff(0)
        tb(0)
        q_ff(0)
        m1(0, 0)
        t_ff(1)
        tb(1)
        regroup_w2(nc.scalar.copy, 1, 0, 3)
        regroup_w2(nc.vector.tensor_copy, 1, 3, 4)
        c_ff(1)
        p1(0, 0)
        quant_w2(1)
        m1(0, 1)
        tb(2)
        p1(0, 1)
        for n in range(0, K - 1):
            if n % 2 == 0:
                p_new = (n + 8) // 2
                if p_new < K // 2:
                    load_ffh(p_new)
                    load_tgt(p_new)
                    load_dup(p_new)
            if n == 0:
                nc.sync.dma_start(out=dbias[:], in_=dup_bias.partition_broadcast(P))
            if n > 0:
                p1(n, 0)
                p1(n, 1)
            if tok(n - 8) and group_start(n - 7) != group_start(n - 8):
                oa(n - 8)
            if n == 0:
                nm(0)
            if tok(n - 1):
                sq(n - 1)
            p_af, i_af = (n - 4) // 2, 2 * (n % 2)
            if p_af >= 0:
                af_pair(p_af, i_af)
            m1(n + 1, 0)
            m1(n + 1, 1)
            if tok(n - 7):
                m2(n - 7)
            if n > 0 and tok(n + 2):
                tb(n + 2)
            if n > 0:
                nm(n)
            if n == 1:
                gain_shift_columns()
            if tok(n - 2):
                xh(n - 2)
            if tok(n - 1):
                sr(n - 1)
            if p_af >= 0:
                af_pair(p_af, i_af + 1)
            if tok(n - 1) and not xh_on_vector(n - 1):
                nbias(n - 1)
            if n % 2 == 1 and tok(n + 3):
                c_ff((n + 3) // 2)
            if n % 2 == 0 and n >= 4:
                tz_pair((n - 4) // 2, 2)
                tz_pair((n - 4) // 2, 3)
            if n % 2 == 1 and n >= 3:
                tz_pair((n - 3) // 2, 0)
                tz_pair((n - 3) // 2, 1)
            if n % 2 == 0 and tok(n + 4):
                t_ff((n + 4) // 2)
            if n % 2 == 0 and tok(n + 2):
                q_ff((n + 2) // 2)
            if tok(n - 6):
                rg_second(n - 6)
            if tok(n - 5):
                rg(n - 5)
            if tok(n - 2):
                qd(n - 2)
            if tok(n - 6):
                qh(n - 6)
            dr(n)
        p1(31, 0)
        p1(31, 1)
        sq(30)
        af_pair(13, 2)
        rg_second(25)
        m2(24)
        xh(29)
        af_pair(13, 3)
        tz(28)
        nm(31)
        sr(30)
        oa(23)
        qd(29)
        rg(26)
        qh(25)
        m2(25)
        rg_second(26)
        rg(27)
        rg_second(27)
        sq(31)
        xh(30)
        tz(29)
        af(28, 0)
        sr(31)
        af(28, 1)
        qh(26)
        m2(26)
        xh(31)
        tz(30)
        rg(28)
        af(29, 0)
        af(29, 1)
        tz(31)
        qh(27)
        m2(27)
        qh(28)
        m2(28)
        qd(30)
        rg(29)
        dr(31)
        qh(29)
        m2(29)
        af(30, 0)
        af(30, 1)
        oa(27)
        rg(30)
        qd(31)
        qh(30)
        m2(30)
        af(31, 0)
        af(31, 1)
        rg(31)
        qh(31)
        m2(31)
        oa(30)
        oa(31)
